import numpy as np
import ml_dtypes


def mxq(x, axis, fmt="e4m3"):
    dtype, down = {"e4m3": (ml_dtypes.float8_e4m3fn, 7), "e5m2": (ml_dtypes.float8_e5m2, 14)}[fmt]
    v = np.moveaxis(np.asarray(x, np.float32).astype(ml_dtypes.bfloat16).astype(np.float64), axis, -1)
    blocks = v.reshape(v.shape[:-1] + (-1, 32))
    amax = np.abs(blocks).max(-1, keepdims=True)
    byte = np.maximum(np.where(amax > 0, np.frexp(amax)[1] - 1 + 127, 0) - down, 1)
    scale = np.exp2(byte - 127.0)
    codes = (blocks / scale).astype(np.float32).astype(dtype).astype(np.float64)
    return np.moveaxis((codes * scale).reshape(v.shape), -1, axis)


WIDE = False


def mx_kscale(k):
    if not WIDE:
        return np.ones(k)
    levels = np.array([10, -10, 5, -5, 0])
    a = np.random.permutation(np.resize(levels, k // 512 * 4)).reshape(k // 512, 4)
    idx = np.arange(k)
    return np.exp2(a[idx // 512, idx % 128 // 32])


BF16 = ml_dtypes.bfloat16


def bf(x):
    return np.asarray(x, np.float32).astype(BF16)


def f64(x):
    return np.asarray(x).astype(np.float64)


B, L, C, KS, NL, BH, R = 1, 128, 512, 4, 24, 64, 4
OUT = 2 * BH * NL


def setup_inputs():
    s, t = mx_kscale(C), mx_kscale(C)
    return {"local_features": bf(np.random.standard_normal((B, L, C)) * s),
            "wt": bf(np.random.standard_normal((C, C, KS)) / np.sqrt(C) / s[:, None, None] * t[None, :, None]),
            "bt": bf(np.random.standard_normal(C) * 0.5 * t),
            "w1": bf(np.random.standard_normal((OUT, C)) / np.sqrt(C) / t[None, :]),
            "b1": bf(np.random.standard_normal(OUT) * 0.5)}


def reference(local_features, wt, bt, w1, b1):
    xq = mxq(f64(local_features), 2, "e4m3")
    wq = mxq(f64(wt), 0, "e4m3")
    up = xq @ wq.reshape(C, C * KS)
    up = up.reshape(B, L, C, KS).transpose(0, 2, 1, 3).reshape(B, C, L * KS) + f64(bt)[None, :, None]
    y = (mxq(f64(w1), 1, "e4m3") @ mxq(up, 1, "e4m3")) + f64(b1)[None, :, None]
    y = np.tile(y, (1, 1, R))
    y = y.reshape(B, NL, 2 * BH, L * KS * R)
    return np.ascontiguousarray(y.transpose(2, 0, 1, 3))

@@ -1,0 +1,219 @@
+from contextlib import ExitStack
+
+import concourse.mybir as mybir
+from concourse.masks import make_identity
+
+BF16 = mybir.dt.bfloat16
+F32 = mybir.dt.float32
+U32 = mybir.dt.uint32
+U8 = mybir.dt.uint8
+FP8X4 = mybir.dt.float8_e4m3fn_x4
+ADD = mybir.AluOpType.add
+IDENTITY = mybir.ActivationFunctionType.Identity
+
+P = 128
+PACK = 4
+HALVES = 2
+PAIR = 2
+L = 128
+C = 512
+TAPS = 4
+T = L * TAPS
+LAYERS = 24
+REPEATS = 4
+WT_COLS = C * TAPS
+W1_ROWS = 4
+GROUP = W1_ROWS
+GROUPS = LAYERS // GROUP
+STORE = 2
+BT_ROW = 32
+
+FLOPS = 2 * L * C * WT_COLS + 2 * LAYERS * P * C * T
+
+
+def tile_conditionalfeaturesupsample_kernel(tc, local_features, wt, bt, w1, b1, out):
+    nc = tc.nc
+    with ExitStack() as ctx:
+        ctx.enter_context(tc.manual_schedule())
+        keep = ctx.enter_context(tc.tile_pool(name="keep", bufs=1))
+        stage = ctx.enter_context(tc.tile_pool(name="stage", bufs=2))
+        results = ctx.enter_context(tc.tile_pool(name="results", bufs=4))
+        word_banks = ctx.enter_context(tc.psum_pool(name="word_banks", bufs=3))
+        sum_banks = ctx.enter_context(tc.psum_pool(name="sum_banks", bufs=5))
+
+        ident = keep.tile([P, P], F32)
+        make_identity(nc, ident[:])
+
+        x_rows = keep.tile([P, C], BF16)
+        nc.sync.dma_start(out=x_rows[:], in_=local_features.rearrange("b l c -> (b l) c"))
+
+        wt_rows = keep.tile([P, PACK, WT_COLS], BF16)
+        wt_matrix = wt.rearrange("c o k -> c (o k)")
+        half_cols = WT_COLS // HALVES
+        for h in range(HALVES):
+            cols = slice(h * half_cols, (h + 1) * half_cols)
+            for u in range(HALVES):
+                nc.sync.dma_start(
+                    out=wt_rows[:, PAIR * u : PAIR * (u + 1), cols],
+                    in_=wt_matrix[u * PAIR * P : (u + 1) * PAIR * P, cols].rearrange(
+                        "(q e) w -> q e w", e=PAIR
+                    ),
+                )
+
+        w1_rows = keep.tile([P, GROUPS, W1_ROWS, C], BF16)
+        for g in range(GROUPS):
+            nc.sync.dma_start(
+                out=w1_rows[:, g],
+                in_=w1[g * GROUP * P : (g + 1) * GROUP * P, :].rearrange(
+                    "(q s) c -> q s c", s=W1_ROWS
+                ),
+            )
+
+        bias_rows = keep.tile([P, P], F32)
+        nc.vector.memset(bias_rows[:], 0.0)
+        b1_rows = keep.tile([LAYERS, P], BF16)
+        nc.scalar.dma_start(out=b1_rows[:], in_=b1.rearrange("(n j) -> n j", j=P))
+        nc.scalar.dma_start(
+            out=bias_rows[BT_ROW : BT_ROW + HALVES, :].bitcast(BF16),
+            in_=bt.rearrange("(u w) -> u w", u=HALVES),
+        )
+
+        x_bank = word_banks.tile([P, T], F32, tag="words")
+        for u in range(HALVES):
+            nc.tensor.transpose(
+                x_bank[:, u * P : (u + 1) * P], x_rows[:].bitcast(F32)[:, u * P : (u + 1) * P], ident[:]
+            )
+        x_grouped = keep.tile([P, L * PACK], BF16, align_bytes=64)
+        nc.vector.tensor_copy(
+            out=x_grouped[:].bitcast(F32).rearrange("p (l u) -> p l u", u=HALVES),
+            in_=x_bank[:, 0 : HALVES * P].rearrange("p (u l) -> p l u", u=HALVES),
+        )
+        nc.vector.tensor_copy(out=bias_rows[0:LAYERS, :], in_=b1_rows[:])
+        x_codes = keep.tile([P, L], U32, align_bytes=64)
+        x_scales = keep.tile([P, L], U8, align_bytes=64)
+        nc.vector.quantize_mx(out=x_codes[:].bitcast(FP8X4), scales=x_scales[:], in_=x_grouped[:])
+
+        bias_bank = word_banks.tile([P, T], F32, tag="words")
+        nc.tensor.transpose(bias_bank[:, 0:P], bias_rows[:], ident[:])
+        b1_col = keep.tile([P, LAYERS], F32)
+        nc.vector.tensor_copy(out=b1_col[:], in_=bias_bank[:, 0:LAYERS])
+        bt_pairs = keep.tile([P, PACK], BF16)
+        nc.vector.tensor_copy(out=bt_pairs[:].bitcast(F32), in_=bias_bank[:, BT_ROW : BT_ROW + HALVES])
+        bt_col = keep.tile([P, PACK], F32)
+        nc.vector.tensor_copy(out=bt_col[:], in_=bt_pairs[:])
+
+        wt_grouped = keep.tile([P, HALVES, PAIR, TAPS, P, PACK], BF16, align_bytes=64)
+        wt_codes = keep.tile([P, HALVES, PAIR, TAPS, P], U32, align_bytes=64)
+        wt_scales = keep.tile([P, HALVES, PAIR, TAPS, P], U8, align_bytes=64)
+        wt_sorted = wt_rows[:].rearrange(
+            "p t (h m e k) -> p h e k m t", h=HALVES, m=P, e=PAIR, k=TAPS
+        )
+        up_banks = []
+        for k in range(TAPS):
+            up_bank = sum_banks.tile([P, T], F32, tag="sums")
+            up_banks.append(up_bank)
+        for h in range(HALVES):
+            nc.vector.tensor_copy(out=wt_grouped[:, h, 0], in_=wt_sorted[:, h, 0])
+            nc.scalar.copy(out=wt_grouped[:, h, 1], in_=wt_sorted[:, h, 1])
+            for e in range(PAIR):
+                nc.vector.quantize_mx(
+                    out=wt_codes[:, h, e].rearrange("p k m -> p (k m)").bitcast(FP8X4),
+                    scales=wt_scales[:, h, e].rearrange("p k m -> p (k m)"),
+                    in_=wt_grouped[:, h, e].rearrange("p k m t -> p (k m t)"),
+                )
+                j = PAIR * h + e
+                for k in range(TAPS):
+                    nc.tensor.matmul_mx(
+                        out=up_banks[k][:, j * L : (j + 1) * L],
+                        lhsT=wt_codes[:, h, e, k].bitcast(FP8X4),
+                        lhsT_scale=wt_scales[:, h, e, k],
+                        rhs=x_codes[:].bitcast(FP8X4),
+                        rhs_scale=x_scales[:],
+                        start=True,
+                        stop=True,
+                    )
+
+        w1_codes = keep.tile([P, LAYERS, P], U32, align_bytes=64)
+        w1_scales = keep.tile([P, LAYERS, P], U8, align_bytes=64)
+
+        def w1_words_to_partitions(g):
+            w1_grouped = stage.tile([P, GROUP * P * PACK], BF16, align_bytes=64)
+            words = w1_grouped[:].bitcast(F32).rearrange("p (q f) -> p q f", f=W1_ROWS * HALVES)
+            per_bank = T // P
+            for first in range(0, W1_ROWS * HALVES, per_bank):
+                w1_bank = word_banks.tile([P, T], F32, tag="words")
+                for f in range(per_bank):
+                    s, u = divmod(first + f, HALVES)
+                    nc.tensor.transpose(
+                        w1_bank[:, f * P : (f + 1) * P],
+                        w1_rows[:, g, s].bitcast(F32)[:, u * P : (u + 1) * P],
+                        ident[:],
+                    )
+                nc.scalar.copy(
+                    out=words[:, :, first : first + per_bank],
+                    in_=w1_bank[:].rearrange("p (f q) -> p q f", f=per_bank),
+                )
+            return w1_grouped
+
+        def w1_quantise(g, w1_grouped):
+            layers = slice(g * GROUP, (g + 1) * GROUP)
+            nc.vector.quantize_mx(
+                out=w1_codes[:, layers].rearrange("p n j -> p (n j)").bitcast(FP8X4),
+                scales=w1_scales[:, layers].rearrange("p n j -> p (n j)"),
+                in_=w1_grouped[:],
+            )
+
+        w1_grouped = w1_words_to_partitions(0)
+
+        up_grouped = keep.tile([P, TAPS, L, PACK], BF16, align_bytes=64)
+        for k in range(TAPS):
+            nc.vector.tensor_tensor(
+                out=up_grouped[:, k],
+                in0=up_banks[k][:].rearrange("p (j l) -> p l j", j=PACK),
+                in1=bt_col[:].unsqueeze(1).to_broadcast([P, L, PACK]),
+                op=ADD,
+            )
+        w1_quantise(0, w1_grouped)
+        up_codes = keep.tile([P, T], U32, align_bytes=64)
+        up_scales = keep.tile([P, T], U8, align_bytes=64)
+        nc.vector.quantize_mx(
+            out=up_codes[:].bitcast(FP8X4),
+            scales=up_scales[:],
+            in_=up_grouped[:].rearrange("p k l j -> p (k l j)"),
+        )
+
+        for g in range(GROUPS):
+            for first in range(g * GROUP, (g + 1) * GROUP, STORE):
+                y_rows = results.tile([P, STORE, REPEATS * T], F32)
+                for i in range(STORE):
+                    n = first + i
+                    y_bank = sum_banks.tile([P, T], F32, tag="sums")
+                    nc.tensor.matmul_mx(
+                        out=y_bank[:],
+                        lhsT=w1_codes[:, n].bitcast(FP8X4),
+                        lhsT_scale=w1_scales[:, n],
+                        rhs=up_codes[:].bitcast(FP8X4),
+                        rhs_scale=up_scales[:],
+                        start=True,
+                        stop=True,
+                    )
+                    repeated = (
+                        y_bank[:]
+                        .rearrange("p (k l) -> p l k", k=TAPS)
+                        .unsqueeze(1)
+                        .to_broadcast([P, REPEATS, L, TAPS])
+                    )
+                    target = y_rows[:, i].rearrange("p (r l k) -> p r l k", r=REPEATS, k=TAPS)
+                    if i % 2 == 0:
+                        nc.scalar.activation(
+                            out=target, in_=repeated, func=IDENTITY, bias=b1_col[:, n : n + 1]
+                        )
+                    else:
+                        nc.vector.tensor_scalar(
+                            out=target, in0=repeated, scalar1=b1_col[:, n : n + 1], scalar2=None, op0=ADD
+                        )
+                nc.sync.dma_start(out=out[:, 0, first : first + STORE, :], in_=y_rows[:])
+                if first == g * GROUP and g + 1 < GROUPS:
+                    w1_grouped = w1_words_to_partitions(g + 1)
+            if g + 1 < GROUPS:
+                w1_quantise(g + 1, w1_grouped)

@@ -106,15 +106,16 @@ def tile_conditionalfeaturesupsample_kernel(tc, local_features, wt, bt, w1, b1, 
         wt_codes = keep.tile([P, HALVES, PAIR, TAPS, P], U32, align_bytes=64)
         wt_scales = keep.tile([P, HALVES, PAIR, TAPS, P], U8, align_bytes=64)
         wt_sorted = wt_rows[:].rearrange(
-            "p t (h m e k) -> p h e k m t", h=HALVES, m=P, e=PAIR, k=TAPS
+            "p t (h m e k) -> p h e m t k", h=HALVES, m=P, e=PAIR, k=TAPS
         )
+        wt_targets = wt_grouped[:].rearrange("p h e k m t -> p h e m t k")
         up_banks = []
         for k in range(TAPS):
             up_bank = sum_banks.tile([P, T], F32, tag="sums")
             up_banks.append(up_bank)
         for h in range(HALVES):
-            nc.vector.tensor_copy(out=wt_grouped[:, h, 0], in_=wt_sorted[:, h, 0])
-            nc.scalar.copy(out=wt_grouped[:, h, 1], in_=wt_sorted[:, h, 1])
+            nc.vector.tensor_copy(out=wt_targets[:, h, 0], in_=wt_sorted[:, h, 0])
+            nc.scalar.copy(out=wt_targets[:, h, 1], in_=wt_sorted[:, h, 1])
             for e in range(PAIR):
                 nc.vector.quantize_mx(
                     out=wt_codes[:, h, e].rearrange("p k m -> p (k m)").bitcast(FP8X4),

@@ -113,17 +113,18 @@ def tile_conditionalfeaturesupsample_kernel(tc, local_features, wt, bt, w1, b1, 
         for k in range(TAPS):
             up_bank = sum_banks.tile([P, T], F32, tag="sums")
             up_banks.append(up_bank)
-        for h in range(HALVES):
+
+        def wt_half(h):
             nc.vector.tensor_copy(out=wt_targets[:, h, 0], in_=wt_sorted[:, h, 0])
             nc.scalar.copy(out=wt_targets[:, h, 1], in_=wt_sorted[:, h, 1])
             for e in range(PAIR):
-                nc.vector.quantize_mx(
-                    out=wt_codes[:, h, e].rearrange("p k m -> p (k m)").bitcast(FP8X4),
-                    scales=wt_scales[:, h, e].rearrange("p k m -> p (k m)"),
-                    in_=wt_grouped[:, h, e].rearrange("p k m t -> p (k m t)"),
-                )
                 j = PAIR * h + e
                 for k in range(TAPS):
+                    nc.vector.quantize_mx(
+                        out=wt_codes[:, h, e, k].bitcast(FP8X4),
+                        scales=wt_scales[:, h, e, k],
+                        in_=wt_grouped[:, h, e, k].rearrange("p m t -> p (m t)"),
+                    )
                     nc.tensor.matmul_mx(
                         out=up_banks[k][:, j * L : (j + 1) * L],
                         lhsT=wt_codes[:, h, e, k].bitcast(FP8X4),
@@ -137,10 +138,10 @@ def tile_conditionalfeaturesupsample_kernel(tc, local_features, wt, bt, w1, b1, 
         w1_codes = keep.tile([P, LAYERS, P], U32, align_bytes=64)
         w1_scales = keep.tile([P, LAYERS, P], U8, align_bytes=64)
 
-        def w1_words_to_partitions(g):
-            w1_grouped = stage.tile([P, GROUP * P * PACK], BF16, align_bytes=64)
-            words = w1_grouped[:].bitcast(F32).rearrange("p (q f) -> p q f", f=W1_ROWS * HALVES)
-            per_bank = T // P
+        per_bank = T // P
+
+        def w1_transposes(g):
+            w1_banks = []
             for first in range(0, W1_ROWS * HALVES, per_bank):
                 w1_bank = word_banks.tile([P, T], F32, tag="words")
                 for f in range(per_bank):
@@ -150,9 +151,16 @@ def tile_conditionalfeaturesupsample_kernel(tc, local_features, wt, bt, w1, b1, 
                         w1_rows[:, g, s].bitcast(F32)[:, u * P : (u + 1) * P],
                         ident[:],
                     )
+                w1_banks.append(w1_bank)
+            return w1_banks
+
+        def w1_copies(w1_banks):
+            w1_grouped = stage.tile([P, GROUP * P * PACK], BF16, align_bytes=64)
+            words = w1_grouped[:].bitcast(F32).rearrange("p (q f) -> p q f", f=W1_ROWS * HALVES)
+            for b in range(len(w1_banks)):
                 nc.scalar.copy(
-                    out=words[:, :, first : first + per_bank],
-                    in_=w1_bank[:].rearrange("p (f q) -> p q f", f=per_bank),
+                    out=words[:, :, b * per_bank : (b + 1) * per_bank],
+                    in_=w1_banks[b][:].rearrange("p (f q) -> p q f", f=per_bank),
                 )
             return w1_grouped
 
@@ -164,7 +172,10 @@ def tile_conditionalfeaturesupsample_kernel(tc, local_features, wt, bt, w1, b1, 
                 in_=w1_grouped[:],
             )
 
-        w1_grouped = w1_words_to_partitions(0)
+        wt_half(0)
+        w1_banks = w1_transposes(0)
+        wt_half(1)
+        w1_grouped = w1_copies(w1_banks)
 
         up_grouped = keep.tile([P, TAPS, L, PACK], BF16, align_bytes=64)
         for k in range(TAPS):
@@ -215,6 +226,6 @@ def tile_conditionalfeaturesupsample_kernel(tc, local_features, wt, bt, w1, b1, 
                         )
                 nc.sync.dma_start(out=out[:, 0, first : first + STORE, :], in_=y_rows[:])
                 if first == g * GROUP and g + 1 < GROUPS:
-                    w1_grouped = w1_words_to_partitions(g + 1)
+                    w1_grouped = w1_copies(w1_transposes(g + 1))
             if g + 1 < GROUPS:
                 w1_quantise(g + 1, w1_grouped)

@@ -22,6 +22,7 @@ T = L * TAPS
 LAYERS = 24
 REPEATS = 4
 WT_COLS = C * TAPS
+PIECES = 2
 W1_ROWS = 4
 GROUP = W1_ROWS
 GROUPS = LAYERS // GROUP
@@ -34,7 +35,6 @@ FLOPS = 2 * L * C * WT_COLS + 2 * LAYERS * P * C * T
 def tile_conditionalfeaturesupsample_kernel(tc, local_features, wt, bt, w1, b1, out):
     nc = tc.nc
     with ExitStack() as ctx:
-        ctx.enter_context(tc.manual_schedule())
         keep = ctx.enter_context(tc.tile_pool(name="keep", bufs=1))
         stage = ctx.enter_context(tc.tile_pool(name="stage", bufs=2))
         results = ctx.enter_context(tc.tile_pool(name="results", bufs=4))
@@ -49,9 +49,9 @@ def tile_conditionalfeaturesupsample_kernel(tc, local_features, wt, bt, w1, b1, 
 
         wt_rows = keep.tile([P, PACK, WT_COLS], BF16)
         wt_matrix = wt.rearrange("c o k -> c (o k)")
-        half_cols = WT_COLS // HALVES
-        for h in range(HALVES):
-            cols = slice(h * half_cols, (h + 1) * half_cols)
+        piece_cols = WT_COLS // (HALVES * PIECES)
+        for piece in range(HALVES * PIECES):
+            cols = slice(piece * piece_cols, (piece + 1) * piece_cols)
             for u in range(HALVES):
                 nc.sync.dma_start(
                     out=wt_rows[:, PAIR * u : PAIR * (u + 1), cols],
@@ -115,8 +115,10 @@ def tile_conditionalfeaturesupsample_kernel(tc, local_features, wt, bt, w1, b1, 
             up_banks.append(up_bank)
 
         def wt_half(h):
-            nc.vector.tensor_copy(out=wt_targets[:, h, 0], in_=wt_sorted[:, h, 0])
-            nc.scalar.copy(out=wt_targets[:, h, 1], in_=wt_sorted[:, h, 1])
+            for piece in range(PIECES):
+                ms = slice(piece * P // PIECES, (piece + 1) * P // PIECES)
+                nc.vector.tensor_copy(out=wt_targets[:, h, 0, ms], in_=wt_sorted[:, h, 0, ms])
+                nc.scalar.copy(out=wt_targets[:, h, 1, ms], in_=wt_sorted[:, h, 1, ms])
             for e in range(PAIR):
                 j = PAIR * h + e
                 for k in range(TAPS):

from contextlib import ExitStack

import concourse.mybir as mybir
from concourse.masks import make_identity

BF16 = mybir.dt.bfloat16
F32 = mybir.dt.float32
U32 = mybir.dt.uint32
U8 = mybir.dt.uint8
FP8X4 = mybir.dt.float8_e4m3fn_x4
ADD = mybir.AluOpType.add
IDENTITY = mybir.ActivationFunctionType.Identity

P = 128
PACK = 4
HALVES = 2
PAIR = 2
L = 128
C = 512
TAPS = 4
T = L * TAPS
LAYERS = 24
REPEATS = 4
WT_COLS = C * TAPS
PIECES = 2
W1_ROWS = 4
GROUP = W1_ROWS
GROUPS = LAYERS // GROUP
STORE = 2
BT_ROW = 32

FLOPS = 2 * L * C * WT_COLS + 2 * LAYERS * P * C * T


def tile_conditionalfeaturesupsample_kernel(tc, local_features, wt, bt, w1, b1, out):
    nc = tc.nc
    with ExitStack() as ctx:
        keep = ctx.enter_context(tc.tile_pool(name="keep", bufs=1))
        stage = ctx.enter_context(tc.tile_pool(name="stage", bufs=2))
        results = ctx.enter_context(tc.tile_pool(name="results", bufs=4))
        word_banks = ctx.enter_context(tc.psum_pool(name="word_banks", bufs=3))
        sum_banks = ctx.enter_context(tc.psum_pool(name="sum_banks", bufs=5))

        ident = keep.tile([P, P], F32)
        make_identity(nc, ident[:])

        x_rows = keep.tile([P, C], BF16)
        nc.sync.dma_start(out=x_rows[:], in_=local_features.rearrange("b l c -> (b l) c"))

        wt_rows = keep.tile([P, PACK, WT_COLS], BF16)
        wt_matrix = wt.rearrange("c o k -> c (o k)")
        piece_cols = WT_COLS // (HALVES * PIECES)
        for piece in range(HALVES * PIECES):
            cols = slice(piece * piece_cols, (piece + 1) * piece_cols)
            for u in range(HALVES):
                nc.sync.dma_start(
                    out=wt_rows[:, PAIR * u : PAIR * (u + 1), cols],
                    in_=wt_matrix[u * PAIR * P : (u + 1) * PAIR * P, cols].rearrange(
                        "(q e) w -> q e w", e=PAIR
                    ),
                )

        w1_rows = keep.tile([P, GROUPS, W1_ROWS, C], BF16)
        for g in range(GROUPS):
            nc.sync.dma_start(
                out=w1_rows[:, g],
                in_=w1[g * GROUP * P : (g + 1) * GROUP * P, :].rearrange(
                    "(q s) c -> q s c", s=W1_ROWS
                ),
            )

        bias_rows = keep.tile([P, P], F32)
        nc.vector.memset(bias_rows[:], 0.0)
        b1_rows = keep.tile([LAYERS, P], BF16)
        nc.scalar.dma_start(out=b1_rows[:], in_=b1.rearrange("(n j) -> n j", j=P))
        nc.scalar.dma_start(
            out=bias_rows[BT_ROW : BT_ROW + HALVES, :].bitcast(BF16),
            in_=bt.rearrange("(u w) -> u w", u=HALVES),
        )

        x_bank = word_banks.tile([P, T], F32, tag="words")
        for u in range(HALVES):
            nc.tensor.transpose(
                x_bank[:, u * P : (u + 1) * P], x_rows[:].bitcast(F32)[:, u * P : (u + 1) * P], ident[:]
            )
        x_grouped = keep.tile([P, L * PACK], BF16, align_bytes=64)
        nc.vector.tensor_copy(
            out=x_grouped[:].bitcast(F32).rearrange("p (l u) -> p l u", u=HALVES),
            in_=x_bank[:, 0 : HALVES * P].rearrange("p (u l) -> p l u", u=HALVES),
        )
        nc.vector.tensor_copy(out=bias_rows[0:LAYERS, :], in_=b1_rows[:])
        x_codes = keep.tile([P, L], U32, align_bytes=64)
        x_scales = keep.tile([P, L], U8, align_bytes=64)
        nc.vector.quantize_mx(out=x_codes[:].bitcast(FP8X4), scales=x_scales[:], in_=x_grouped[:])

        bias_bank = word_banks.tile([P, T], F32, tag="words")
        nc.tensor.transpose(bias_bank[:, 0:P], bias_rows[:], ident[:])
        b1_col = keep.tile([P, LAYERS], F32)
        nc.vector.tensor_copy(out=b1_col[:], in_=bias_bank[:, 0:LAYERS])
        bt_pairs = keep.tile([P, PACK], BF16)
        nc.vector.tensor_copy(out=bt_pairs[:].bitcast(F32), in_=bias_bank[:, BT_ROW : BT_ROW + HALVES])
        bt_col = keep.tile([P, PACK], F32)
        nc.vector.tensor_copy(out=bt_col[:], in_=bt_pairs[:])

        wt_grouped = keep.tile([P, HALVES, PAIR, TAPS, P, PACK], BF16, align_bytes=64)
        wt_codes = keep.tile([P, HALVES, PAIR, TAPS, P], U32, align_bytes=64)
        wt_scales = keep.tile([P, HALVES, PAIR, TAPS, P], U8, align_bytes=64)
        wt_sorted = wt_rows[:].rearrange(
            "p t (h m e k) -> p h e m t k", h=HALVES, m=P, e=PAIR, k=TAPS
        )
        wt_targets = wt_grouped[:].rearrange("p h e k m t -> p h e m t k")
        up_banks = []
        for k in range(TAPS):
            up_bank = sum_banks.tile([P, T], F32, tag="sums")
            up_banks.append(up_bank)

        def wt_half(h):
            for piece in range(PIECES):
                ms = slice(piece * P // PIECES, (piece + 1) * P // PIECES)
                nc.vector.tensor_copy(out=wt_targets[:, h, 0, ms], in_=wt_sorted[:, h, 0, ms])
                nc.scalar.copy(out=wt_targets[:, h, 1, ms], in_=wt_sorted[:, h, 1, ms])
            for e in range(PAIR):
                j = PAIR * h + e
                for k in range(TAPS):
                    nc.vector.quantize_mx(
                        out=wt_codes[:, h, e, k].bitcast(FP8X4),
                        scales=wt_scales[:, h, e, k],
                        in_=wt_grouped[:, h, e, k].rearrange("p m t -> p (m t)"),
                    )
                    nc.tensor.matmul_mx(
                        out=up_banks[k][:, j * L : (j + 1) * L],
                        lhsT=wt_codes[:, h, e, k].bitcast(FP8X4),
                        lhsT_scale=wt_scales[:, h, e, k],
                        rhs=x_codes[:].bitcast(FP8X4),
                        rhs_scale=x_scales[:],
                        start=True,
                        stop=True,
                    )

        w1_codes = keep.tile([P, LAYERS, P], U32, align_bytes=64)
        w1_scales = keep.tile([P, LAYERS, P], U8, align_bytes=64)

        per_bank = T // P

        def w1_transposes(g):
            w1_banks = []
            for first in range(0, W1_ROWS * HALVES, per_bank):
                w1_bank = word_banks.tile([P, T], F32, tag="words")
                for f in range(per_bank):
                    s, u = divmod(first + f, HALVES)
                    nc.tensor.transpose(
                        w1_bank[:, f * P : (f + 1) * P],
                        w1_rows[:, g, s].bitcast(F32)[:, u * P : (u + 1) * P],
                        ident[:],
                    )
                w1_banks.append(w1_bank)
            return w1_banks

        def w1_copies(w1_banks):
            w1_grouped = stage.tile([P, GROUP * P * PACK], BF16, align_bytes=64)
            words = w1_grouped[:].bitcast(F32).rearrange("p (q f) -> p q f", f=W1_ROWS * HALVES)
            for b in range(len(w1_banks)):
                nc.scalar.copy(
                    out=words[:, :, b * per_bank : (b + 1) * per_bank],
                    in_=w1_banks[b][:].rearrange("p (f q) -> p q f", f=per_bank),
                )
            return w1_grouped

        def w1_quantise(g, w1_grouped):
            layers = slice(g * GROUP, (g + 1) * GROUP)
            nc.vector.quantize_mx(
                out=w1_codes[:, layers].rearrange("p n j -> p (n j)").bitcast(FP8X4),
                scales=w1_scales[:, layers].rearrange("p n j -> p (n j)"),
                in_=w1_grouped[:],
            )

        wt_half(0)
        w1_banks = w1_transposes(0)
        wt_half(1)
        w1_grouped = w1_copies(w1_banks)

        up_grouped = keep.tile([P, TAPS, L, PACK], BF16, align_bytes=64)
        for k in range(TAPS):
            nc.vector.tensor_tensor(
                out=up_grouped[:, k],
                in0=up_banks[k][:].rearrange("p (j l) -> p l j", j=PACK),
                in1=bt_col[:].unsqueeze(1).to_broadcast([P, L, PACK]),
                op=ADD,
            )
        w1_quantise(0, w1_grouped)
        up_codes = keep.tile([P, T], U32, align_bytes=64)
        up_scales = keep.tile([P, T], U8, align_bytes=64)
        nc.vector.quantize_mx(
            out=up_codes[:].bitcast(FP8X4),
            scales=up_scales[:],
            in_=up_grouped[:].rearrange("p k l j -> p (k l j)"),
        )

        for g in range(GROUPS):
            for first in range(g * GROUP, (g + 1) * GROUP, STORE):
                y_rows = results.tile([P, STORE, REPEATS * T], F32)
                for i in range(STORE):
                    n = first + i
                    y_bank = sum_banks.tile([P, T], F32, tag="sums")
                    nc.tensor.matmul_mx(
                        out=y_bank[:],
                        lhsT=w1_codes[:, n].bitcast(FP8X4),
                        lhsT_scale=w1_scales[:, n],
                        rhs=up_codes[:].bitcast(FP8X4),
                        rhs_scale=up_scales[:],
                        start=True,
                        stop=True,
                    )
                    repeated = (
                        y_bank[:]
                        .rearrange("p (k l) -> p l k", k=TAPS)
                        .unsqueeze(1)
                        .to_broadcast([P, REPEATS, L, TAPS])
                    )
                    target = y_rows[:, i].rearrange("p (r l k) -> p r l k", r=REPEATS, k=TAPS)
                    if i % 2 == 0:
                        nc.scalar.activation(
                            out=target, in_=repeated, func=IDENTITY, bias=b1_col[:, n : n + 1]
                        )
                    else:
                        nc.vector.tensor_scalar(
                            out=target, in0=repeated, scalar1=b1_col[:, n : n + 1], scalar2=None, op0=ADD
                        )
                nc.sync.dma_start(out=out[:, 0, first : first + STORE, :], in_=y_rows[:])
                if first == g * GROUP and g + 1 < GROUPS:
                    w1_grouped = w1_copies(w1_transposes(g + 1))
            if g + 1 < GROUPS:
                w1_quantise(g + 1, w1_grouped)
